import numpy as np
import ml_dtypes

BF16 = ml_dtypes.bfloat16


def bf(x):
    return np.asarray(x, np.float32).astype(BF16)


def f32(x):
    return np.asarray(x, np.float32)


def f64(x):
    return np.asarray(x).astype(np.float64)


def striped(idx):
    return np.tile(idx.reshape(-1, 16).T, (8, 1))


S, D, M, L, N = 1024, 128, 128, 128, 128
LN_EPS = 1e-6


def setup_inputs():
    return {"table": bf(np.random.standard_normal((S, D))), "w1": bf(np.random.standard_normal((D, M)) / np.sqrt(D)), "b1": f32(0.1 * np.random.standard_normal((M, 1))), "ln_scale": f32(1.0 + 0.1 * np.random.standard_normal((M, 1))), "ln_bias": f32(0.1 * np.random.standard_normal((M, 1))), "w4": bf(np.random.standard_normal((M, L)) / np.sqrt(M)), "b4": f32(0.1 * np.random.standard_normal((L, 1))), "offs": striped(np.random.permutation(np.tile(np.arange(S), 2))[:N])}


def reference(table, w1, b1, ln_scale, ln_bias, w4, b4, offs):
    idx = offs[:16].T.reshape(-1)
    u = f64(w1).T @ f64(table)[idx].T + f64(b1)
    mu = u.mean(axis=0, keepdims=True)
    var = np.square(u - mu).mean(axis=0, keepdims=True)
    h = np.maximum((u - mu) / np.sqrt(var + LN_EPS) * f64(ln_scale) + f64(ln_bias), 0.0)
    return np.exp(f64(w4).T @ h + f64(b4))

@@ -1,0 +1,113 @@
+import concourse.mybir as mybir
+from concourse.masks import make_identity
+
+P = 128
+GENES = 1024
+CELLS = 128
+PIECES = 4
+PIECE_BLOCKS = GENES // P // PIECES
+PIECE_GENES = PIECE_BLOCKS * P
+LN_EPS = 1e-6
+
+FLOPS = 2 * P * P * CELLS + 2 * P * P * CELLS
+BYTES = CELLS * P * 2 + 2 * P * P * 2 + 4 * P * 4 + P * (CELLS // 16) * 2 + P * CELLS * 4
+
+BF16 = mybir.dt.bfloat16
+F32 = mybir.dt.float32
+U16 = mybir.dt.uint16
+ACT = mybir.ActivationFunctionType
+ALU = mybir.AluOpType
+
+
+def tile_gibbsencoder_kernel(tc, table, w1, b1, ln_scale, ln_bias, w4, b4, offs, out):
+    nc = tc.nc
+    with (
+        tc.tile_pool(name="held", bufs=1) as held,
+        tc.psum_pool(name="flip", bufs=PIECES) as flip,
+        tc.psum_pool(name="chain", bufs=1) as chain,
+    ):
+        b1_sb = held.tile([P, 1], F32, name="b1_sb")
+        with nc.allow_non_contiguous_dma(reason="one float to a partition"):
+            nc.scalar.dma_start(b1_sb[:], b1)
+        w1_sb = held.tile([P, P], BF16, name="w1_sb")
+        nc.scalar.dma_start(w1_sb[:], w1)
+        table_blocks = table.rearrange("(b p) d -> p b d", p=P)
+        rows = []
+        for piece in range(PIECES):
+            rows_piece = held.tile([P, PIECE_BLOCKS, P], BF16, name=f"rows{piece}")
+            nc.sync.dma_start(
+                rows_piece[:],
+                table_blocks[:, piece * PIECE_BLOCKS : (piece + 1) * PIECE_BLOCKS, :],
+            )
+            rows.append(rows_piece)
+        offsets = held.tile([P, CELLS // 16], U16, name="offsets")
+        nc.sync.dma_start(offsets[:], offs)
+        scale_sb = held.tile([P, 1], F32, name="scale_sb")
+        bias_sb = held.tile([P, 1], F32, name="bias_sb")
+        w4_sb = held.tile([P, P], BF16, name="w4_sb")
+        b4_sb = held.tile([P, 1], F32, name="b4_sb")
+        with nc.allow_non_contiguous_dma(reason="one float to a partition"):
+            nc.sync.dma_start(scale_sb[:], ln_scale)
+            nc.sync.dma_start(bias_sb[:], ln_bias)
+            nc.sync.dma_start(w4_sb[:], w4)
+            nc.sync.dma_start(b4_sb[:], b4)
+
+        ident_bf = held.tile([P, P], BF16, name="ident_bf")
+        make_identity(nc, ident_bf[:])
+        mean_weights = held.tile([P, P], F32, name="mean_weights")
+        nc.vector.memset(mean_weights[:], 1.0 / P)
+        eps = held.tile([P, 1], F32, name="eps")
+        nc.vector.memset(eps[:], LN_EPS)
+        warm = held.tile([P, 1], F32, name="warm")
+        nc.scalar.activation(warm[:], eps[:], ACT.Abs_reciprocal_sqrt)
+
+        b1_mean_ps = chain.tile([P, 1], F32, name="b1_mean_ps")
+        nc.tensor.matmul(b1_mean_ps[:], mean_weights[:], b1_sb[:], start=True, stop=True)
+        b1c = held.tile([P, 1], F32, name="b1c")
+        nc.vector.tensor_tensor(b1c[:], b1_sb[:], b1_mean_ps[:], ALU.subtract)
+        w1_over_p = held.tile([P, P], F32, name="w1_over_p")
+        w1_mean = held.tile([P, 1], F32, name="w1_mean")
+        nc.scalar.activation(w1_over_p[:], w1_sb[:], ACT.Copy, scale=1.0 / P, accum_out=w1_mean[:])
+        w1c_hi = held.tile([P, P], BF16, name="w1c_hi")
+        nc.vector.tensor_scalar_sub(w1c_hi[:], w1_sb[:], w1_mean[:])
+        w1c_lo = held.tile([P, P], BF16, name="w1c_lo")
+        nc.vector.scalar_tensor_tensor(
+            w1c_lo[:], w1_sb[:], w1_mean[:], w1c_hi[:], ALU.subtract, ALU.subtract
+        )
+
+        window = held.tile([P, GENES], BF16, name="window")
+        for piece in range(PIECES):
+            flipped = flip.tile([P, PIECE_GENES], BF16, name="flipped")
+            for block in range(PIECE_BLOCKS):
+                nc.tensor.transpose(
+                    flipped[:, block * P : (block + 1) * P], rows[piece][:, block, :], ident_bf[:]
+                )
+            window_part = window[:, piece * PIECE_GENES : (piece + 1) * PIECE_GENES]
+            if piece % 2 == 0:
+                nc.vector.tensor_copy(window_part, flipped[:])
+            else:
+                nc.scalar.copy(window_part, flipped[:])
+
+        uc_ps = chain.tile([P, CELLS], F32, name="uc_ps")
+        nc.tensor.matmul(uc_ps[:], w1c_hi[:], window[:].indirect(offsets[:]), start=True, stop=False)
+        nc.tensor.matmul(uc_ps[:], w1c_lo[:], window[:].indirect(offsets[:]), start=False, stop=True)
+
+        squares = held.tile([P, CELLS], F32, name="squares")
+        nc.scalar.activation(squares[:], uc_ps[:], ACT.Square, bias=b1c[:])
+        var_ps = chain.tile([P, CELLS], F32, name="var_ps")
+        nc.tensor.matmul(var_ps[:], mean_weights[:], squares[:], start=True, stop=True)
+        gained = held.tile([P, CELLS], F32, name="gained")
+        nc.vector.tensor_scalar(gained[:], uc_ps[:], b1c[:], scale_sb[:], ALU.add, ALU.mult)
+        rstd = held.tile([P, CELLS], F32, name="rstd")
+        nc.scalar.activation(rstd[:], var_ps[:], ACT.Abs_reciprocal_sqrt, bias=eps[:])
+
+        normed = held.tile([P, CELLS], F32, name="normed")
+        nc.vector.tensor_tensor(normed[:], gained[:], rstd[:], ALU.mult)
+        h = held.tile([P, CELLS], BF16, name="h")
+        nc.vector.tensor_scalar(h[:], normed[:], bias_sb[:], 0.0, ALU.add, ALU.max)
+
+        o_ps = chain.tile([P, CELLS], F32, name="o_ps")
+        nc.tensor.matmul(o_ps[:], w4_sb[:], h[:], start=True, stop=True)
+        result = held.tile([P, CELLS], F32, name="result")
+        nc.scalar.activation(result[:], o_ps[:], ACT.Exp, bias=b4_sb[:])
+        nc.sync.dma_start(out, result[:])

@@ -61,10 +61,6 @@ def tile_gibbsencoder_kernel(tc, table, w1, b1, ln_scale, ln_bias, w4, b4, offs,
         warm = held.tile([P, 1], F32, name="warm")
         nc.scalar.activation(warm[:], eps[:], ACT.Abs_reciprocal_sqrt)
 
-        b1_mean_ps = chain.tile([P, 1], F32, name="b1_mean_ps")
-        nc.tensor.matmul(b1_mean_ps[:], mean_weights[:], b1_sb[:], start=True, stop=True)
-        b1c = held.tile([P, 1], F32, name="b1c")
-        nc.vector.tensor_tensor(b1c[:], b1_sb[:], b1_mean_ps[:], ALU.subtract)
         w1_over_p = held.tile([P, P], F32, name="w1_over_p")
         w1_mean = held.tile([P, 1], F32, name="w1_mean")
         nc.scalar.activation(w1_over_p[:], w1_sb[:], ACT.Copy, scale=1.0 / P, accum_out=w1_mean[:])
@@ -87,6 +83,11 @@ def tile_gibbsencoder_kernel(tc, table, w1, b1, ln_scale, ln_bias, w4, b4, offs,
                 nc.vector.tensor_copy(window_part, flipped[:])
             else:
                 nc.scalar.copy(window_part, flipped[:])
+
+        b1_mean_ps = flip.tile([P, 1], F32, name="b1_mean_ps", tag="flipped")
+        nc.tensor.matmul(b1_mean_ps[:], mean_weights[:], b1_sb[:], start=True, stop=True)
+        b1c = held.tile([P, 1], F32, name="b1c")
+        nc.vector.tensor_tensor(b1c[:], b1_sb[:], b1_mean_ps[:], ALU.subtract)
 
         uc_ps = chain.tile([P, CELLS], F32, name="uc_ps")
         nc.tensor.matmul(uc_ps[:], w1c_hi[:], window[:].indirect(offsets[:]), start=True, stop=False)

@@ -23,7 +23,7 @@ def tile_gibbsencoder_kernel(tc, table, w1, b1, ln_scale, ln_bias, w4, b4, offs,
     nc = tc.nc
     with (
         tc.tile_pool(name="held", bufs=1) as held,
-        tc.psum_pool(name="flip", bufs=PIECES) as flip,
+        tc.psum_pool(name="flip", bufs=1) as flip,
         tc.psum_pool(name="chain", bufs=1) as chain,
     ):
         b1_sb = held.tile([P, 1], F32, name="b1_sb")
@@ -56,6 +56,8 @@ def tile_gibbsencoder_kernel(tc, table, w1, b1, ln_scale, ln_bias, w4, b4, offs,
         make_identity(nc, ident_bf[:])
         mean_weights = held.tile([P, P], F32, name="mean_weights")
         nc.vector.memset(mean_weights[:], 1.0 / P)
+        mean_weights_bf = held.tile([P, P], BF16, name="mean_weights_bf")
+        nc.vector.memset(mean_weights_bf[:], 1.0 / P)
         eps = held.tile([P, 1], F32, name="eps")
         nc.vector.memset(eps[:], LN_EPS)
         warm = held.tile([P, 1], F32, name="warm")
@@ -73,7 +75,7 @@ def tile_gibbsencoder_kernel(tc, table, w1, b1, ln_scale, ln_bias, w4, b4, offs,
 
         window = held.tile([P, GENES], BF16, name="window")
         for piece in range(PIECES):
-            flipped = flip.tile([P, PIECE_GENES], BF16, name="flipped")
+            flipped = flip.tile([P, PIECE_GENES], BF16, name=f"flipped{piece}")
             for block in range(PIECE_BLOCKS):
                 nc.tensor.transpose(
                     flipped[:, block * P : (block + 1) * P], rows[piece][:, block, :], ident_bf[:]
@@ -84,10 +86,15 @@ def tile_gibbsencoder_kernel(tc, table, w1, b1, ln_scale, ln_bias, w4, b4, offs,
             else:
                 nc.scalar.copy(window_part, flipped[:])
 
-        b1_mean_ps = flip.tile([P, 1], F32, name="b1_mean_ps", tag="flipped")
-        nc.tensor.matmul(b1_mean_ps[:], mean_weights[:], b1_sb[:], start=True, stop=True)
+        b1_parts = held.tile([P, 2], BF16, name="b1_parts")
+        nc.gpsimd.tensor_copy(b1_parts[:, 0:1], b1_sb[:])
+        nc.gpsimd.tensor_tensor(b1_parts[:, 1:2], b1_sb[:], b1_parts[:, 0:1], ALU.subtract)
+        b1_means_ps = flip.tile([P, 2], F32, name="b1_means_ps", tag="flipped1")
+        nc.tensor.matmul(b1_means_ps[:], mean_weights_bf[:], b1_parts[:], start=True, stop=True)
         b1c = held.tile([P, 1], F32, name="b1c")
-        nc.vector.tensor_tensor(b1c[:], b1_sb[:], b1_mean_ps[:], ALU.subtract)
+        nc.vector.scalar_tensor_tensor(
+            b1c[:], b1_sb[:], b1_means_ps[:, 0:1], b1_means_ps[:, 1:2], ALU.subtract, ALU.subtract
+        )
 
         uc_ps = chain.tile([P, CELLS], F32, name="uc_ps")
         nc.tensor.matmul(uc_ps[:], w1c_hi[:], window[:].indirect(offsets[:]), start=True, stop=False)

@@ -89,7 +89,7 @@ def tile_gibbsencoder_kernel(tc, table, w1, b1, ln_scale, ln_bias, w4, b4, offs,
         b1_parts = held.tile([P, 2], BF16, name="b1_parts")
         nc.gpsimd.tensor_copy(b1_parts[:, 0:1], b1_sb[:])
         nc.gpsimd.tensor_tensor(b1_parts[:, 1:2], b1_sb[:], b1_parts[:, 0:1], ALU.subtract)
-        b1_means_ps = flip.tile([P, 2], F32, name="b1_means_ps", tag="flipped1")
+        b1_means_ps = flip.tile([P, 2], F32, name="b1_means_ps", tag="flipped2")
         nc.tensor.matmul(b1_means_ps[:], mean_weights_bf[:], b1_parts[:], start=True, stop=True)
         b1c = held.tile([P, 1], F32, name="b1c")
         nc.vector.scalar_tensor_tensor(

@@ -26,9 +26,6 @@ def tile_gibbsencoder_kernel(tc, table, w1, b1, ln_scale, ln_bias, w4, b4, offs,
         tc.psum_pool(name="flip", bufs=1) as flip,
         tc.psum_pool(name="chain", bufs=1) as chain,
     ):
-        b1_sb = held.tile([P, 1], F32, name="b1_sb")
-        with nc.allow_non_contiguous_dma(reason="one float to a partition"):
-            nc.scalar.dma_start(b1_sb[:], b1)
         w1_sb = held.tile([P, P], BF16, name="w1_sb")
         nc.scalar.dma_start(w1_sb[:], w1)
         table_blocks = table.rearrange("(b p) d -> p b d", p=P)
@@ -42,11 +39,13 @@ def tile_gibbsencoder_kernel(tc, table, w1, b1, ln_scale, ln_bias, w4, b4, offs,
             rows.append(rows_piece)
         offsets = held.tile([P, CELLS // 16], U16, name="offsets")
         nc.sync.dma_start(offsets[:], offs)
+        b1_sb = held.tile([P, 1], F32, name="b1_sb")
         scale_sb = held.tile([P, 1], F32, name="scale_sb")
         bias_sb = held.tile([P, 1], F32, name="bias_sb")
         w4_sb = held.tile([P, P], BF16, name="w4_sb")
         b4_sb = held.tile([P, 1], F32, name="b4_sb")
         with nc.allow_non_contiguous_dma(reason="one float to a partition"):
+            nc.sync.dma_start(b1_sb[:], b1)
             nc.sync.dma_start(scale_sb[:], ln_scale)
             nc.sync.dma_start(bias_sb[:], ln_bias)
             nc.sync.dma_start(w4_sb[:], w4)

@@ -26,6 +26,9 @@ def tile_gibbsencoder_kernel(tc, table, w1, b1, ln_scale, ln_bias, w4, b4, offs,
         tc.psum_pool(name="flip", bufs=1) as flip,
         tc.psum_pool(name="chain", bufs=1) as chain,
     ):
+        b1_sb = held.tile([P, 1], F32, name="b1_sb")
+        with nc.allow_non_contiguous_dma(reason="one float to a partition"):
+            nc.scalar.dma_start(b1_sb[:], b1)
         w1_sb = held.tile([P, P], BF16, name="w1_sb")
         nc.scalar.dma_start(w1_sb[:], w1)
         table_blocks = table.rearrange("(b p) d -> p b d", p=P)
@@ -39,13 +42,11 @@ def tile_gibbsencoder_kernel(tc, table, w1, b1, ln_scale, ln_bias, w4, b4, offs,
             rows.append(rows_piece)
         offsets = held.tile([P, CELLS // 16], U16, name="offsets")
         nc.sync.dma_start(offsets[:], offs)
-        b1_sb = held.tile([P, 1], F32, name="b1_sb")
         scale_sb = held.tile([P, 1], F32, name="scale_sb")
         bias_sb = held.tile([P, 1], F32, name="bias_sb")
         w4_sb = held.tile([P, P], BF16, name="w4_sb")
         b4_sb = held.tile([P, 1], F32, name="b4_sb")
         with nc.allow_non_contiguous_dma(reason="one float to a partition"):
-            nc.sync.dma_start(b1_sb[:], b1)
             nc.sync.dma_start(scale_sb[:], ln_scale)
             nc.sync.dma_start(bias_sb[:], ln_bias)
             nc.sync.dma_start(w4_sb[:], w4)
@@ -53,10 +54,8 @@ def tile_gibbsencoder_kernel(tc, table, w1, b1, ln_scale, ln_bias, w4, b4, offs,
 
         ident_bf = held.tile([P, P], BF16, name="ident_bf")
         make_identity(nc, ident_bf[:])
-        mean_weights = held.tile([P, P], F32, name="mean_weights")
+        mean_weights = held.tile([P, P], BF16, name="mean_weights")
         nc.vector.memset(mean_weights[:], 1.0 / P)
-        mean_weights_bf = held.tile([P, P], BF16, name="mean_weights_bf")
-        nc.vector.memset(mean_weights_bf[:], 1.0 / P)
         eps = held.tile([P, 1], F32, name="eps")
         nc.vector.memset(eps[:], LN_EPS)
         warm = held.tile([P, 1], F32, name="warm")
@@ -89,7 +88,7 @@ def tile_gibbsencoder_kernel(tc, table, w1, b1, ln_scale, ln_bias, w4, b4, offs,
         nc.gpsimd.tensor_copy(b1_parts[:, 0:1], b1_sb[:])
         nc.gpsimd.tensor_tensor(b1_parts[:, 1:2], b1_sb[:], b1_parts[:, 0:1], ALU.subtract)
         b1_means_ps = flip.tile([P, 2], F32, name="b1_means_ps", tag="flipped2")
-        nc.tensor.matmul(b1_means_ps[:], mean_weights_bf[:], b1_parts[:], start=True, stop=True)
+        nc.tensor.matmul(b1_means_ps[:], mean_weights[:], b1_parts[:], start=True, stop=True)
         b1c = held.tile([P, 1], F32, name="b1c")
         nc.vector.scalar_tensor_tensor(
             b1c[:], b1_sb[:], b1_means_ps[:, 0:1], b1_means_ps[:, 1:2], ALU.subtract, ALU.subtract
@@ -101,15 +100,28 @@ def tile_gibbsencoder_kernel(tc, table, w1, b1, ln_scale, ln_bias, w4, b4, offs,
 
         squares = held.tile([P, CELLS], F32, name="squares")
         nc.scalar.activation(squares[:], uc_ps[:], ACT.Square, bias=b1c[:])
+        upper_halves = squares[:].bitcast(BF16)[:, 1::2]
         var_ps = chain.tile([P, CELLS], F32, name="var_ps")
-        nc.tensor.matmul(var_ps[:], mean_weights[:], squares[:], start=True, stop=True)
+        nc.tensor.matmul(var_ps[:], mean_weights[:], upper_halves, start=True, stop=True)
+        rest = held.tile([P, CELLS], BF16, name="rest")
+        nc.vector.tensor_tensor(rest[:], squares[:], upper_halves, ALU.subtract)
+        rest_ps = chain.tile([P, CELLS], F32, name="rest_ps")
+        nc.tensor.matmul(rest_ps[:], mean_weights[:], rest[:], start=True, stop=True)
         gained = held.tile([P, CELLS], F32, name="gained")
         nc.vector.tensor_scalar(gained[:], uc_ps[:], b1c[:], scale_sb[:], ALU.add, ALU.mult)
+
         rstd = held.tile([P, CELLS], F32, name="rstd")
         nc.scalar.activation(rstd[:], var_ps[:], ACT.Abs_reciprocal_sqrt, bias=eps[:])
-
+        slope = held.tile([P, CELLS], F32, name="slope")
+        nc.vector.scalar_tensor_tensor(slope[:], rstd[:], -0.5, rstd[:], ALU.mult, ALU.mult)
+        nearly_normed = held.tile([P, CELLS], F32, name="nearly_normed")
+        nc.vector.tensor_tensor(nearly_normed[:], gained[:], rstd[:], ALU.mult)
+        correction = held.tile([P, CELLS], F32, name="correction")
+        nc.vector.tensor_tensor(correction[:], rest_ps[:], slope[:], ALU.mult)
         normed = held.tile([P, CELLS], F32, name="normed")
-        nc.vector.tensor_tensor(normed[:], gained[:], rstd[:], ALU.mult)
+        nc.vector.scalar_tensor_tensor(
+            normed[:], correction[:], 1.0, nearly_normed[:], ALU.add, ALU.mult
+        )
         h = held.tile([P, CELLS], BF16, name="h")
         nc.vector.tensor_scalar(h[:], normed[:], bias_sb[:], 0.0, ALU.add, ALU.max)
 

@@ -113,17 +113,31 @@ def tile_gibbsencoder_kernel(tc, table, w1, b1, ln_scale, ln_bias, w4, b4, offs,
         rstd = held.tile([P, CELLS], F32, name="rstd")
         nc.scalar.activation(rstd[:], var_ps[:], ACT.Abs_reciprocal_sqrt, bias=eps[:])
         slope = held.tile([P, CELLS], F32, name="slope")
-        nc.vector.scalar_tensor_tensor(slope[:], rstd[:], -0.5, rstd[:], ALU.mult, ALU.mult)
         nearly_normed = held.tile([P, CELLS], F32, name="nearly_normed")
-        nc.vector.tensor_tensor(nearly_normed[:], gained[:], rstd[:], ALU.mult)
         correction = held.tile([P, CELLS], F32, name="correction")
-        nc.vector.tensor_tensor(correction[:], rest_ps[:], slope[:], ALU.mult)
         normed = held.tile([P, CELLS], F32, name="normed")
-        nc.vector.scalar_tensor_tensor(
-            normed[:], correction[:], 1.0, nearly_normed[:], ALU.add, ALU.mult
-        )
         h = held.tile([P, CELLS], BF16, name="h")
-        nc.vector.tensor_scalar(h[:], normed[:], bias_sb[:], 0.0, ALU.add, ALU.max)
+        halves = [slice(0, CELLS // 2), slice(CELLS // 2, CELLS)]
+        for half in halves:
+            nc.vector.scalar_tensor_tensor(
+                slope[:, half], rstd[:, half], -0.5, rstd[:, half], ALU.mult, ALU.mult
+            )
+        for half in halves:
+            nc.vector.tensor_tensor(
+                correction[:, half], rest_ps[:, half], slope[:, half], ALU.mult
+            )
+        for half in halves:
+            nc.vector.tensor_tensor(
+                nearly_normed[:, half], gained[:, half], rstd[:, half], ALU.mult
+            )
+        for half in halves:
+            nc.vector.scalar_tensor_tensor(
+                normed[:, half], correction[:, half], 1.0, nearly_normed[:, half], ALU.add, ALU.mult
+            )
+        for half in halves:
+            nc.vector.tensor_scalar(
+                h[:, half], normed[:, half], bias_sb[:], 0.0, ALU.add, ALU.max
+            )
 
         o_ps = chain.tile([P, CELLS], F32, name="o_ps")
         nc.tensor.matmul(o_ps[:], w4_sb[:], h[:], start=True, stop=True)

@@ -4,9 +4,7 @@ from concourse.masks import make_identity
 P = 128
 GENES = 1024
 CELLS = 128
-PIECES = 4
-PIECE_BLOCKS = GENES // P // PIECES
-PIECE_GENES = PIECE_BLOCKS * P
+PIECE_BLOCKS = (2, 3, 2, 1)
 LN_EPS = 1e-6
 
 FLOPS = 2 * P * P * CELLS + 2 * P * P * CELLS
@@ -33,12 +31,10 @@ def tile_gibbsencoder_kernel(tc, table, w1, b1, ln_scale, ln_bias, w4, b4, offs,
         nc.scalar.dma_start(w1_sb[:], w1)
         table_blocks = table.rearrange("(b p) d -> p b d", p=P)
         rows = []
-        for piece in range(PIECES):
-            rows_piece = held.tile([P, PIECE_BLOCKS, P], BF16, name=f"rows{piece}")
-            nc.sync.dma_start(
-                rows_piece[:],
-                table_blocks[:, piece * PIECE_BLOCKS : (piece + 1) * PIECE_BLOCKS, :],
-            )
+        for piece, blocks in enumerate(PIECE_BLOCKS):
+            first = sum(PIECE_BLOCKS[:piece])
+            rows_piece = held.tile([P, blocks, P], BF16, name=f"rows{piece}")
+            nc.sync.dma_start(rows_piece[:], table_blocks[:, first : first + blocks, :])
             rows.append(rows_piece)
         offsets = held.tile([P, CELLS // 16], U16, name="offsets")
         nc.sync.dma_start(offsets[:], offs)
@@ -72,13 +68,14 @@ def tile_gibbsencoder_kernel(tc, table, w1, b1, ln_scale, ln_bias, w4, b4, offs,
         )
 
         window = held.tile([P, GENES], BF16, name="window")
-        for piece in range(PIECES):
-            flipped = flip.tile([P, PIECE_GENES], BF16, name=f"flipped{piece}")
-            for block in range(PIECE_BLOCKS):
+        for piece, blocks in enumerate(PIECE_BLOCKS):
+            flipped = flip.tile([P, blocks * P], BF16, name=f"flipped{piece}")
+            for block in range(blocks):
                 nc.tensor.transpose(
                     flipped[:, block * P : (block + 1) * P], rows[piece][:, block, :], ident_bf[:]
                 )
-            window_part = window[:, piece * PIECE_GENES : (piece + 1) * PIECE_GENES]
+            first = sum(PIECE_BLOCKS[:piece])
+            window_part = window[:, first * P : (first + blocks) * P]
             if piece % 2 == 0:
                 nc.vector.tensor_copy(window_part, flipped[:])
             else:
@@ -98,11 +95,19 @@ def tile_gibbsencoder_kernel(tc, table, w1, b1, ln_scale, ln_bias, w4, b4, offs,
         nc.tensor.matmul(uc_ps[:], w1c_hi[:], window[:].indirect(offsets[:]), start=True, stop=False)
         nc.tensor.matmul(uc_ps[:], w1c_lo[:], window[:].indirect(offsets[:]), start=False, stop=True)
 
+        halves = [slice(0, CELLS // 2), slice(CELLS // 2, CELLS)]
         squares = held.tile([P, CELLS], F32, name="squares")
-        nc.scalar.activation(squares[:], uc_ps[:], ACT.Square, bias=b1c[:])
         upper_halves = squares[:].bitcast(BF16)[:, 1::2]
-        var_ps = chain.tile([P, CELLS], F32, name="var_ps")
-        nc.tensor.matmul(var_ps[:], mean_weights[:], upper_halves, start=True, stop=True)
+        rstd = held.tile([P, CELLS], F32, name="rstd")
+        var_banks = []
+        for half in halves:
+            nc.scalar.activation(squares[:, half], uc_ps[:, half], ACT.Square, bias=b1c[:])
+        for number, half in enumerate(halves):
+            var_ps = chain.tile([P, CELLS // 2], F32, name=f"var{number}_ps")
+            nc.tensor.matmul(
+                var_ps[:], mean_weights[:], upper_halves[:, half], start=True, stop=True
+            )
+            var_banks.append(var_ps)
         rest = held.tile([P, CELLS], BF16, name="rest")
         nc.vector.tensor_tensor(rest[:], squares[:], upper_halves, ALU.subtract)
         rest_ps = chain.tile([P, CELLS], F32, name="rest_ps")
@@ -110,14 +115,13 @@ def tile_gibbsencoder_kernel(tc, table, w1, b1, ln_scale, ln_bias, w4, b4, offs,
         gained = held.tile([P, CELLS], F32, name="gained")
         nc.vector.tensor_scalar(gained[:], uc_ps[:], b1c[:], scale_sb[:], ALU.add, ALU.mult)
 
-        rstd = held.tile([P, CELLS], F32, name="rstd")
-        nc.scalar.activation(rstd[:], var_ps[:], ACT.Abs_reciprocal_sqrt, bias=eps[:])
+        for var_ps, half in zip(var_banks, halves):
+            nc.scalar.activation(rstd[:, half], var_ps[:], ACT.Abs_reciprocal_sqrt, bias=eps[:])
         slope = held.tile([P, CELLS], F32, name="slope")
         nearly_normed = held.tile([P, CELLS], F32, name="nearly_normed")
         correction = held.tile([P, CELLS], F32, name="correction")
         normed = held.tile([P, CELLS], F32, name="normed")
         h = held.tile([P, CELLS], BF16, name="h")
-        halves = [slice(0, CELLS // 2), slice(CELLS // 2, CELLS)]
         for half in halves:
             nc.vector.scalar_tensor_tensor(
                 slope[:, half], rstd[:, half], -0.5, rstd[:, half], ALU.mult, ALU.mult
@@ -139,8 +143,9 @@ def tile_gibbsencoder_kernel(tc, table, w1, b1, ln_scale, ln_bias, w4, b4, offs,
                 h[:, half], normed[:, half], bias_sb[:], 0.0, ALU.add, ALU.max
             )
 
-        o_ps = chain.tile([P, CELLS], F32, name="o_ps")
-        nc.tensor.matmul(o_ps[:], w4_sb[:], h[:], start=True, stop=True)
+        o_ps = flip.tile([P, CELLS], F32, name="o_ps", tag="flipped0")
+        for half in halves:
+            nc.tensor.matmul(o_ps[:, half], w4_sb[:], h[:, half], start=True, stop=True)
         result = held.tile([P, CELLS], F32, name="result")
         nc.scalar.activation(result[:], o_ps[:], ACT.Exp, bias=b4_sb[:])
         nc.sync.dma_start(out, result[:])

@@ -24,11 +24,11 @@ def tile_gibbsencoder_kernel(tc, table, w1, b1, ln_scale, ln_bias, w4, b4, offs,
         tc.psum_pool(name="flip", bufs=1) as flip,
         tc.psum_pool(name="chain", bufs=1) as chain,
     ):
+        w1_sb = held.tile([P, P], BF16, name="w1_sb")
+        nc.scalar.dma_start(w1_sb[:], w1)
         b1_sb = held.tile([P, 1], F32, name="b1_sb")
         with nc.allow_non_contiguous_dma(reason="one float to a partition"):
             nc.scalar.dma_start(b1_sb[:], b1)
-        w1_sb = held.tile([P, P], BF16, name="w1_sb")
-        nc.scalar.dma_start(w1_sb[:], w1)
         table_blocks = table.rearrange("(b p) d -> p b d", p=P)
         rows = []
         for piece, blocks in enumerate(PIECE_BLOCKS):

import concourse.mybir as mybir
from concourse.masks import make_identity

P = 128
GENES = 1024
CELLS = 128
PIECE_BLOCKS = (2, 3, 2, 1)
LN_EPS = 1e-6

FLOPS = 2 * P * P * CELLS + 2 * P * P * CELLS
BYTES = CELLS * P * 2 + 2 * P * P * 2 + 4 * P * 4 + P * (CELLS // 16) * 2 + P * CELLS * 4

BF16 = mybir.dt.bfloat16
F32 = mybir.dt.float32
U16 = mybir.dt.uint16
ACT = mybir.ActivationFunctionType
ALU = mybir.AluOpType


def tile_gibbsencoder_kernel(tc, table, w1, b1, ln_scale, ln_bias, w4, b4, offs, out):
    nc = tc.nc
    with (
        tc.tile_pool(name="held", bufs=1) as held,
        tc.psum_pool(name="flip", bufs=1) as flip,
        tc.psum_pool(name="chain", bufs=1) as chain,
    ):
        w1_sb = held.tile([P, P], BF16, name="w1_sb")
        nc.scalar.dma_start(w1_sb[:], w1)
        b1_sb = held.tile([P, 1], F32, name="b1_sb")
        with nc.allow_non_contiguous_dma(reason="one float to a partition"):
            nc.scalar.dma_start(b1_sb[:], b1)
        table_blocks = table.rearrange("(b p) d -> p b d", p=P)
        rows = []
        for piece, blocks in enumerate(PIECE_BLOCKS):
            first = sum(PIECE_BLOCKS[:piece])
            rows_piece = held.tile([P, blocks, P], BF16, name=f"rows{piece}")
            nc.sync.dma_start(rows_piece[:], table_blocks[:, first : first + blocks, :])
            rows.append(rows_piece)
        offsets = held.tile([P, CELLS // 16], U16, name="offsets")
        nc.sync.dma_start(offsets[:], offs)
        scale_sb = held.tile([P, 1], F32, name="scale_sb")
        bias_sb = held.tile([P, 1], F32, name="bias_sb")
        w4_sb = held.tile([P, P], BF16, name="w4_sb")
        b4_sb = held.tile([P, 1], F32, name="b4_sb")
        with nc.allow_non_contiguous_dma(reason="one float to a partition"):
            nc.sync.dma_start(scale_sb[:], ln_scale)
            nc.sync.dma_start(bias_sb[:], ln_bias)
            nc.sync.dma_start(w4_sb[:], w4)
            nc.sync.dma_start(b4_sb[:], b4)

        ident_bf = held.tile([P, P], BF16, name="ident_bf")
        make_identity(nc, ident_bf[:])
        mean_weights = held.tile([P, P], BF16, name="mean_weights")
        nc.vector.memset(mean_weights[:], 1.0 / P)
        eps = held.tile([P, 1], F32, name="eps")
        nc.vector.memset(eps[:], LN_EPS)
        warm = held.tile([P, 1], F32, name="warm")
        nc.scalar.activation(warm[:], eps[:], ACT.Abs_reciprocal_sqrt)

        w1_over_p = held.tile([P, P], F32, name="w1_over_p")
        w1_mean = held.tile([P, 1], F32, name="w1_mean")
        nc.scalar.activation(w1_over_p[:], w1_sb[:], ACT.Copy, scale=1.0 / P, accum_out=w1_mean[:])
        w1c_hi = held.tile([P, P], BF16, name="w1c_hi")
        nc.vector.tensor_scalar_sub(w1c_hi[:], w1_sb[:], w1_mean[:])
        w1c_lo = held.tile([P, P], BF16, name="w1c_lo")
        nc.vector.scalar_tensor_tensor(
            w1c_lo[:], w1_sb[:], w1_mean[:], w1c_hi[:], ALU.subtract, ALU.subtract
        )

        window = held.tile([P, GENES], BF16, name="window")
        for piece, blocks in enumerate(PIECE_BLOCKS):
            flipped = flip.tile([P, blocks * P], BF16, name=f"flipped{piece}")
            for block in range(blocks):
                nc.tensor.transpose(
                    flipped[:, block * P : (block + 1) * P], rows[piece][:, block, :], ident_bf[:]
                )
            first = sum(PIECE_BLOCKS[:piece])
            window_part = window[:, first * P : (first + blocks) * P]
            if piece % 2 == 0:
                nc.vector.tensor_copy(window_part, flipped[:])
            else:
                nc.scalar.copy(window_part, flipped[:])

        b1_parts = held.tile([P, 2], BF16, name="b1_parts")
        nc.gpsimd.tensor_copy(b1_parts[:, 0:1], b1_sb[:])
        nc.gpsimd.tensor_tensor(b1_parts[:, 1:2], b1_sb[:], b1_parts[:, 0:1], ALU.subtract)
        b1_means_ps = flip.tile([P, 2], F32, name="b1_means_ps", tag="flipped2")
        nc.tensor.matmul(b1_means_ps[:], mean_weights[:], b1_parts[:], start=True, stop=True)
        b1c = held.tile([P, 1], F32, name="b1c")
        nc.vector.scalar_tensor_tensor(
            b1c[:], b1_sb[:], b1_means_ps[:, 0:1], b1_means_ps[:, 1:2], ALU.subtract, ALU.subtract
        )

        uc_ps = chain.tile([P, CELLS], F32, name="uc_ps")
        nc.tensor.matmul(uc_ps[:], w1c_hi[:], window[:].indirect(offsets[:]), start=True, stop=False)
        nc.tensor.matmul(uc_ps[:], w1c_lo[:], window[:].indirect(offsets[:]), start=False, stop=True)

        halves = [slice(0, CELLS // 2), slice(CELLS // 2, CELLS)]
        squares = held.tile([P, CELLS], F32, name="squares")
        upper_halves = squares[:].bitcast(BF16)[:, 1::2]
        rstd = held.tile([P, CELLS], F32, name="rstd")
        var_banks = []
        for half in halves:
            nc.scalar.activation(squares[:, half], uc_ps[:, half], ACT.Square, bias=b1c[:])
        for number, half in enumerate(halves):
            var_ps = chain.tile([P, CELLS // 2], F32, name=f"var{number}_ps")
            nc.tensor.matmul(
                var_ps[:], mean_weights[:], upper_halves[:, half], start=True, stop=True
            )
            var_banks.append(var_ps)
        rest = held.tile([P, CELLS], BF16, name="rest")
        nc.vector.tensor_tensor(rest[:], squares[:], upper_halves, ALU.subtract)
        rest_ps = chain.tile([P, CELLS], F32, name="rest_ps")
        nc.tensor.matmul(rest_ps[:], mean_weights[:], rest[:], start=True, stop=True)
        gained = held.tile([P, CELLS], F32, name="gained")
        nc.vector.tensor_scalar(gained[:], uc_ps[:], b1c[:], scale_sb[:], ALU.add, ALU.mult)

        for var_ps, half in zip(var_banks, halves):
            nc.scalar.activation(rstd[:, half], var_ps[:], ACT.Abs_reciprocal_sqrt, bias=eps[:])
        slope = held.tile([P, CELLS], F32, name="slope")
        nearly_normed = held.tile([P, CELLS], F32, name="nearly_normed")
        correction = held.tile([P, CELLS], F32, name="correction")
        normed = held.tile([P, CELLS], F32, name="normed")
        h = held.tile([P, CELLS], BF16, name="h")
        for half in halves:
            nc.vector.scalar_tensor_tensor(
                slope[:, half], rstd[:, half], -0.5, rstd[:, half], ALU.mult, ALU.mult
            )
        for half in halves:
            nc.vector.tensor_tensor(
                correction[:, half], rest_ps[:, half], slope[:, half], ALU.mult
            )
        for half in halves:
            nc.vector.tensor_tensor(
                nearly_normed[:, half], gained[:, half], rstd[:, half], ALU.mult
            )
        for half in halves:
            nc.vector.scalar_tensor_tensor(
                normed[:, half], correction[:, half], 1.0, nearly_normed[:, half], ALU.add, ALU.mult
            )
        for half in halves:
            nc.vector.tensor_scalar(
                h[:, half], normed[:, half], bias_sb[:], 0.0, ALU.add, ALU.max
            )

        o_ps = flip.tile([P, CELLS], F32, name="o_ps", tag="flipped0")
        for half in halves:
            nc.tensor.matmul(o_ps[:, half], w4_sb[:], h[:, half], start=True, stop=True)
        result = held.tile([P, CELLS], F32, name="result")
        nc.scalar.activation(result[:], o_ps[:], ACT.Exp, bias=b4_sb[:])
        nc.sync.dma_start(out, result[:])
